import numpy as np
import ml_dtypes


def mxq(x, axis, fmt="e4m3"):
    dtype, down = {"e4m3": (ml_dtypes.float8_e4m3fn, 7), "e5m2": (ml_dtypes.float8_e5m2, 14)}[fmt]
    v = np.moveaxis(np.asarray(x, np.float32).astype(ml_dtypes.bfloat16).astype(np.float64), axis, -1)
    blocks = v.reshape(v.shape[:-1] + (-1, 32))
    amax = np.abs(blocks).max(-1, keepdims=True)
    byte = np.maximum(np.where(amax > 0, np.frexp(amax)[1] - 1 + 127, 0) - down, 1)
    scale = np.exp2(byte - 127.0)
    codes = (blocks / scale).astype(np.float32).astype(dtype).astype(np.float64)
    return np.moveaxis((codes * scale).reshape(v.shape), -1, axis)


WIDE = False


def mx_kscale(k):
    if not WIDE:
        return np.ones(k)
    levels = np.array([10, -10, 5, -5, 0])
    a = np.random.permutation(np.resize(levels, k // 512 * 4)).reshape(k // 512, 4)
    idx = np.arange(k)
    return np.exp2(a[idx // 512, idx % 128 // 32])


BF16 = ml_dtypes.bfloat16


def bf(x):
    return np.asarray(x, np.float32).astype(BF16)


def f64(x):
    return np.asarray(x).astype(np.float64)


E2M1 = np.array([0.0, 0.5, 1.0, 1.5, 2.0, 3.0, 4.0, 6.0, -0.0, -0.5, -1.0, -1.5, -2.0, -3.0, -4.0, -6.0])


def pack_weight(w, fmt):
    k, n = w.shape
    w = f64(bf(w)).reshape(k // 32, 32, n)
    amax = np.abs(w).max(1)
    if fmt == "e4m3":
        byte = np.frexp(amax)[1] - 1 + 127 - 7
    else:
        mant, ex = np.frexp(amax / 6.0)
        byte = np.where(mant > 0.5, ex, ex - 1) + 127
    byte = np.clip(np.where(amax > 0, byte, 1), 1, 254)
    scaled = (w * np.exp2(127.0 - byte)[:, None, :]).reshape(k, n).astype(np.float32)
    by_word = np.ascontiguousarray(scaled.reshape(k // 512, 128, 4, n).transpose(0, 1, 3, 2))
    if fmt == "e4m3":
        words = by_word.astype(ml_dtypes.float8_e4m3fn).view(np.uint8)
    else:
        c = by_word.astype(ml_dtypes.float4_e2m1fn).view(np.uint8) & 0xF
        words = c[..., 0::2] | (c[..., 1::2] << 4)
    return np.ascontiguousarray(words), np.ascontiguousarray(byte.astype(np.uint8).reshape(k // 512, 16, n))


def unpack_weight(words, scales, fmt):
    g, p, n, _ = words.shape
    if fmt == "e4m3":
        vals = np.ascontiguousarray(words).view(ml_dtypes.float8_e4m3fn).astype(np.float64)
    else:
        nib = np.empty((g, p, n, 4), np.uint8)
        nib[..., 0::2] = words & 0xF
        nib[..., 1::2] = words >> 4
        vals = E2M1[nib]
    vals = vals * np.repeat(np.exp2(scales.astype(np.float64) - 127.0), 8, axis=1)[..., None]
    return vals.transpose(0, 1, 3, 2).reshape(g * 512, n)

def pack4(w):
    words, scales = pack_weight(w, "e2m1")
    return words.reshape(words.shape[0], 128, -1), scales


def unpack4(words, scales):
    return unpack_weight(words.reshape(words.shape[0], 128, -1, 2), scales, "e2m1")


B, N, W, H, D = 1, 16, 512, 4, 128
C = H * D


def setup_inputs():
    t = mx_kscale(C)
    q_feat = bf(np.maximum(np.random.standard_normal((B, H, N, W, D)) * 0.5, 0.0))
    kv_mix = bf(np.random.standard_normal((B, H, N, D, D)) * 0.27 * np.sqrt(W / (2.0 * N)) * t.reshape(H, D)[None, :, None, None, :])
    words, scales = pack4(np.random.standard_normal((C, C)) * 0.5 / np.sqrt(C) / t[:, None])
    b_out = bf(np.random.standard_normal(C) * 0.3)
    return {"q_feat": q_feat,
            "kv_mix": kv_mix,
            "w_out_words": words,
            "w_out_scales": scales,
            "b_out": b_out}


def reference(q_feat, kv_mix, w_out_words, w_out_scales, b_out):
    o = f64(q_feat) @ f64(kv_mix)
    o = o.transpose(0, 2, 3, 1, 4).reshape(B, N, W, C)
    return (mxq(o, 3, "e4m3") @ unpack4(w_out_words, w_out_scales)) + f64(b_out)

@@ -1,0 +1,182 @@
+from contextlib import ExitStack
+
+import concourse.mybir as mybir
+from concourse.masks import make_identity
+
+BF16 = mybir.dt.bfloat16
+F32 = mybir.dt.float32
+I32 = mybir.dt.int32
+U32 = mybir.dt.uint32
+U8 = mybir.dt.uint8
+FP8X4 = mybir.dt.float8_e4m3fn_x4
+FP4X4 = mybir.dt.float4_e2m1fn_x4
+
+P = 128
+HEADS = 4
+WINDOWS = 16
+POSITIONS = 512
+HEAD_DIM = 128
+CHANNELS = HEADS * HEAD_DIM
+ROW_BLOCKS = POSITIONS // P
+PACK = 4
+PAIRS = 2
+HALF = ROW_BLOCKS // 2
+RESULT_BUFS = 12
+
+FLOPS = 2 * HEADS * WINDOWS * POSITIONS * HEAD_DIM * HEAD_DIM + 2 * WINDOWS * POSITIONS * CHANNELS * CHANNELS
+
+
+def tile_mhla_pb_t_kernel(tc, q_feat, kv_mix, w_out_words, w_out_scales, b_out, out):
+    nc = tc.nc
+    with ExitStack() as ctx:
+        ctx.enter_context(tc.manual_schedule())
+        consts = ctx.enter_context(tc.tile_pool(name="consts", bufs=1))
+        inputs = ctx.enter_context(tc.tile_pool(name="inputs", bufs=WINDOWS))
+        work = ctx.enter_context(tc.tile_pool(name="work", bufs=2))
+        results = ctx.enter_context(tc.tile_pool(name="results", bufs=RESULT_BUFS))
+        psum_q = ctx.enter_context(tc.psum_pool(name="psum_q", bufs=2))
+        psum_o = ctx.enter_context(tc.psum_pool(name="psum_o", bufs=2))
+        psum_m = ctx.enter_context(tc.psum_pool(name="psum_m", bufs=2))
+        psum_out = ctx.enter_context(tc.psum_pool(name="psum_out", bufs=2))
+
+        ident_bf16 = consts.tile([P, P], BF16)
+        make_identity(nc, ident_bf16[:])
+        ident_f32 = consts.tile([P, P], F32)
+        make_identity(nc, ident_f32[:])
+
+        bias_row = consts.tile([P, CHANNELS], BF16)
+        nc.vector.memset(bias_row[:], 0.0)
+        ones = consts.tile([P, P], BF16)
+        nc.vector.memset(ones[:], 1.0)
+        nc.sync.dma_start(out=bias_row[0:1, :], in_=b_out.unsqueeze(0))
+
+        w_words = consts.tile([P, 2 * CHANNELS], U8, align_bytes=64)
+        w_scales = consts.tile([P, CHANNELS], U8, align_bytes=64)
+        nc.vector.memset(w_scales[:].bitcast(I32), 0)
+
+        q_rows = []
+        kv_sorted = []
+        for n in range(WINDOWS):
+            kv_tile = inputs.tile([P, HEADS, HEAD_DIM], BF16)
+            nc.sync.dma_start(out=kv_tile[:], in_=kv_mix[0, :, n].rearrange("h d e -> d h e"))
+            q_tile = inputs.tile([P, HEADS, ROW_BLOCKS * HEAD_DIM], BF16)
+            nc.sync.dma_start(
+                out=q_tile[:], in_=q_feat[0, :, n].rearrange("h (r s) d -> r h (s d)", s=ROW_BLOCKS)
+            )
+            q_rows.append(q_tile)
+            if n == 1:
+                nc.sync.dma_start(out=w_words[:].bitcast(I32), in_=w_out_words[0].bitcast(I32))
+                for quadrant in range(4):
+                    nc.sync.dma_start(
+                        out=w_scales[32 * quadrant : 32 * quadrant + 4, :].bitcast(I32),
+                        in_=w_out_scales[0, 4 * quadrant : 4 * quadrant + 4, :].bitcast(I32),
+                    )
+            sorted_tile = inputs.tile([P, HEADS, HEAD_DIM], BF16)
+            nc.gpsimd.tensor_copy(
+                out=sorted_tile[:].bitcast(F32).rearrange("p h (u j) -> p h u j", u=PAIRS),
+                in_=kv_tile[:].bitcast(F32).rearrange("p h (j u) -> p h u j", u=PAIRS),
+            )
+            kv_sorted.append(sorted_tile)
+
+        out_ps = psum_out.tile([P, CHANNELS], F32)
+        nc.tensor.matmul(out=out_ps[:], lhsT=ones[:], rhs=bias_row[:], start=True, stop=True)
+        bias_all = consts.tile([P, CHANNELS], F32)
+        nc.vector.tensor_copy(out=bias_all[:], in_=out_ps[:])
+
+        q_cols = {}
+        m_rows = {}
+        m_cols = {}
+        m_codes = {}
+
+        def transpose_queries(n):
+            qT = work.tile([P, ROW_BLOCKS * HEADS, P], BF16)
+            for half in range(2):
+                qT_ps = psum_q.tile([P, HALF * HEADS, P], BF16)
+                for k in range(HALF * HEADS):
+                    s, h = half * HALF + k // HEADS, k % HEADS
+                    nc.tensor.transpose(
+                        qT_ps[:, k, :], q_rows[n][:, h, s * HEAD_DIM : (s + 1) * HEAD_DIM], ident_bf16[:]
+                    )
+                nc.scalar.copy(out=qT[:, half * HALF * HEADS : (half + 1) * HALF * HEADS, :], in_=qT_ps[:])
+            q_cols[n] = qT
+
+        def first_matmul(n, s, o_ps):
+            for h in range(HEADS):
+                nc.tensor.matmul(
+                    out=o_ps[:, s % HALF, :, h, :],
+                    lhsT=q_cols[n][:, s * HEADS + h, :],
+                    rhs=kv_sorted[n][:, h, :].rearrange("p (u c) -> p u c", u=PAIRS),
+                    start=True,
+                    stop=True,
+                )
+
+        def transpose_merged(n):
+            grouped = work.tile([P, ROW_BLOCKS, P, PACK], BF16, align_bytes=64)
+            for half in range(2):
+                mT_ps = psum_m.tile([P, HALF, PAIRS, P], F32)
+                for k in range(HALF):
+                    words = m_rows[n][:, half * HALF + k, :].bitcast(F32)
+                    for u in range(PAIRS):
+                        nc.tensor.transpose(mT_ps[:, k, u, :], words[:, u * P : (u + 1) * P], ident_f32[:])
+                nc.scalar.copy(
+                    out=grouped[:, half * HALF : (half + 1) * HALF, :, :].bitcast(F32),
+                    in_=mT_ps[:].rearrange("p s u r -> p s r u"),
+                )
+            m_cols[n] = grouped
+
+        def quantise(n):
+            codes = work.tile([P, POSITIONS], U32, align_bytes=64)
+            scales = work.tile([P, POSITIONS], U8, align_bytes=64)
+            nc.vector.quantize_mx(
+                out=codes[:].bitcast(FP8X4),
+                scales=scales[:],
+                in_=m_cols[n][:].rearrange("p s r t -> p (s r t)"),
+            )
+            m_codes[n] = (codes, scales)
+
+        def second_matmul(n, s, result):
+            codes, scales = m_codes[n]
+            cols = slice(s * P, (s + 1) * P)
+            out_ps = psum_out.tile([P, CHANNELS], F32)
+            nc.tensor.matmul_mx(
+                out=out_ps[:],
+                lhsT=codes[:, cols].bitcast(FP8X4),
+                lhsT_scale=scales[:, cols],
+                rhs=w_words[:].bitcast(FP4X4),
+                rhs_scale=w_scales[:],
+                start=True,
+                stop=True,
+            )
+            nc.vector.tensor_tensor(
+                out=result[:, s % HALF, :], in0=out_ps[:], in1=bias_all[:], op=mybir.AluOpType.add
+            )
+
+        for i in range(WINDOWS + 3):
+            n_q, n_first, n_m, n_second = i, i - 1, i - 2, i - 3
+            if n_q < WINDOWS:
+                transpose_queries(n_q)
+            if 0 <= n_m < WINDOWS:
+                transpose_merged(n_m)
+            if 0 <= n_second:
+                quantise(n_second)
+            for half in range(2):
+                if 0 <= n_first < WINDOWS:
+                    o_ps = psum_o.tile([P, HALF, PAIRS, HEADS, HEAD_DIM // PAIRS], BF16)
+                    if half == 0:
+                        merged = work.tile([P, ROW_BLOCKS, CHANNELS], BF16)
+                        m_rows[n_first] = merged
+                if 0 <= n_second:
+                    result = results.tile([P, HALF, CHANNELS], F32)
+                for s in range(half * HALF, (half + 1) * HALF):
+                    if 0 <= n_first < WINDOWS:
+                        first_matmul(n_first, s, o_ps)
+                    if 0 <= n_second:
+                        second_matmul(n_second, s, result)
+                if 0 <= n_first < WINDOWS:
+                    nc.scalar.copy(
+                        out=m_rows[n_first][:, half * HALF : (half + 1) * HALF, :],
+                        in_=o_ps[:].rearrange("p s u h c -> p s (u h c)"),
+                    )
+                if 0 <= n_second:
+                    rows = out[0, n_second].rearrange("(r s) c -> r s c", s=ROW_BLOCKS)
+                    nc.sync.dma_start(out=rows[:, half * HALF : (half + 1) * HALF, :], in_=result[:])

@@ -34,10 +34,8 @@ def tile_mhla_pb_t_kernel(tc, q_feat, kv_mix, w_out_words, w_out_scales, b_out, 
         inputs = ctx.enter_context(tc.tile_pool(name="inputs", bufs=WINDOWS))
         work = ctx.enter_context(tc.tile_pool(name="work", bufs=2))
         results = ctx.enter_context(tc.tile_pool(name="results", bufs=RESULT_BUFS))
-        psum_q = ctx.enter_context(tc.psum_pool(name="psum_q", bufs=2))
-        psum_o = ctx.enter_context(tc.psum_pool(name="psum_o", bufs=2))
-        psum_m = ctx.enter_context(tc.psum_pool(name="psum_m", bufs=2))
-        psum_out = ctx.enter_context(tc.psum_pool(name="psum_out", bufs=2))
+        psum_stage = ctx.enter_context(tc.psum_pool(name="psum_stage", bufs=4))
+        psum_out = ctx.enter_context(tc.psum_pool(name="psum_out", bufs=ROW_BLOCKS))
 
         ident_bf16 = consts.tile([P, P], BF16)
         make_identity(nc, ident_bf16[:])
@@ -91,7 +89,7 @@ def tile_mhla_pb_t_kernel(tc, q_feat, kv_mix, w_out_words, w_out_scales, b_out, 
         def transpose_queries(n):
             qT = work.tile([P, ROW_BLOCKS * HEADS, P], BF16)
             for half in range(2):
-                qT_ps = psum_q.tile([P, HALF * HEADS, P], BF16)
+                qT_ps = psum_stage.tile([P, HALF * HEADS, P], BF16, tag="stage")
                 for k in range(HALF * HEADS):
                     s, h = half * HALF + k // HEADS, k % HEADS
                     nc.tensor.transpose(
@@ -113,7 +111,7 @@ def tile_mhla_pb_t_kernel(tc, q_feat, kv_mix, w_out_words, w_out_scales, b_out, 
         def transpose_merged(n):
             grouped = work.tile([P, ROW_BLOCKS, P, PACK], BF16, align_bytes=64)
             for half in range(2):
-                mT_ps = psum_m.tile([P, HALF, PAIRS, P], F32)
+                mT_ps = psum_stage.tile([P, HALF, PAIRS, P], F32, tag="stage")
                 for k in range(HALF):
                     words = m_rows[n][:, half * HALF + k, :].bitcast(F32)
                     for u in range(PAIRS):
@@ -157,11 +155,11 @@ def tile_mhla_pb_t_kernel(tc, q_feat, kv_mix, w_out_words, w_out_scales, b_out, 
                 transpose_queries(n_q)
             if 0 <= n_m < WINDOWS:
                 transpose_merged(n_m)
-            if 0 <= n_second:
-                quantise(n_second)
             for half in range(2):
+                if half == 1 and 0 <= n_m < WINDOWS:
+                    quantise(n_m)
                 if 0 <= n_first < WINDOWS:
-                    o_ps = psum_o.tile([P, HALF, PAIRS, HEADS, HEAD_DIM // PAIRS], BF16)
+                    o_ps = psum_stage.tile([P, HALF, PAIRS, HEADS, HEAD_DIM // PAIRS], BF16, tag="stage")
                     if half == 0:
                         merged = work.tile([P, ROW_BLOCKS, CHANNELS], BF16)
                         m_rows[n_first] = merged

@@ -86,27 +86,21 @@ def tile_mhla_pb_t_kernel(tc, q_feat, kv_mix, w_out_words, w_out_scales, b_out, 
         m_cols = {}
         m_codes = {}
 
-        def transpose_queries(n):
-            qT = work.tile([P, ROW_BLOCKS * HEADS, P], BF16)
-            for half in range(2):
-                qT_ps = psum_stage.tile([P, HALF * HEADS, P], BF16, tag="stage")
-                for k in range(HALF * HEADS):
-                    s, h = half * HALF + k // HEADS, k % HEADS
-                    nc.tensor.transpose(
-                        qT_ps[:, k, :], q_rows[n][:, h, s * HEAD_DIM : (s + 1) * HEAD_DIM], ident_bf16[:]
-                    )
-                nc.scalar.copy(out=qT[:, half * HALF * HEADS : (half + 1) * HALF * HEADS, :], in_=qT_ps[:])
-            q_cols[n] = qT
+        def transpose_query_block(n, s, h, qT_ps):
+            nc.tensor.transpose(
+                qT_ps[:, (s % HALF) * HEADS + h, :],
+                q_rows[n][:, h, s * HEAD_DIM : (s + 1) * HEAD_DIM],
+                ident_bf16[:],
+            )
 
-        def first_matmul(n, s, o_ps):
-            for h in range(HEADS):
-                nc.tensor.matmul(
-                    out=o_ps[:, s % HALF, :, h, :],
-                    lhsT=q_cols[n][:, s * HEADS + h, :],
-                    rhs=kv_sorted[n][:, h, :].rearrange("p (u c) -> p u c", u=PAIRS),
-                    start=True,
-                    stop=True,
-                )
+        def first_matmul(n, s, h, o_ps):
+            nc.tensor.matmul(
+                out=o_ps[:, s % HALF, :, h, :],
+                lhsT=q_cols[n][:, s * HEADS + h, :],
+                rhs=kv_sorted[n][:, h, :].rearrange("p (u c) -> p u c", u=PAIRS),
+                start=True,
+                stop=True,
+            )
 
         def transpose_merged(n):
             grouped = work.tile([P, ROW_BLOCKS, P, PACK], BF16, align_bytes=64)
@@ -151,30 +145,44 @@ def tile_mhla_pb_t_kernel(tc, q_feat, kv_mix, w_out_words, w_out_scales, b_out, 
 
         for i in range(WINDOWS + 3):
             n_q, n_first, n_m, n_second = i, i - 1, i - 2, i - 3
-            if n_q < WINDOWS:
-                transpose_queries(n_q)
-            if 0 <= n_m < WINDOWS:
+            has_q, has_first = n_q < WINDOWS, 0 <= n_first < WINDOWS
+            has_m, has_second = 0 <= n_m < WINDOWS, 0 <= n_second
+
+            if has_m:
                 transpose_merged(n_m)
+                quantise(n_m)
+
+            if has_q:
+                qT = work.tile([P, ROW_BLOCKS * HEADS, P], BF16)
+                q_cols[n_q] = qT
+            if has_first:
+                merged = work.tile([P, ROW_BLOCKS, CHANNELS], BF16)
+                m_rows[n_first] = merged
             for half in range(2):
-                if half == 1 and 0 <= n_m < WINDOWS:
-                    quantise(n_m)
-                if 0 <= n_first < WINDOWS:
+                blocks = slice(half * HALF, (half + 1) * HALF)
+                if has_q:
+                    qT_ps = psum_stage.tile([P, HALF * HEADS, P], BF16, tag="stage")
+                if has_first:
                     o_ps = psum_stage.tile([P, HALF, PAIRS, HEADS, HEAD_DIM // PAIRS], BF16, tag="stage")
-                    if half == 0:
-                        merged = work.tile([P, ROW_BLOCKS, CHANNELS], BF16)
-                        m_rows[n_first] = merged
-                if 0 <= n_second:
-                    result = results.tile([P, HALF, CHANNELS], F32)
                 for s in range(half * HALF, (half + 1) * HALF):
-                    if 0 <= n_first < WINDOWS:
-                        first_matmul(n_first, s, o_ps)
-                    if 0 <= n_second:
-                        second_matmul(n_second, s, result)
-                if 0 <= n_first < WINDOWS:
+                    for h in range(HEADS):
+                        if has_q:
+                            transpose_query_block(n_q, s, h, qT_ps)
+                        if has_first:
+                            first_matmul(n_first, s, h, o_ps)
+                if has_first:
                     nc.scalar.copy(
-                        out=m_rows[n_first][:, half * HALF : (half + 1) * HALF, :],
-                        in_=o_ps[:].rearrange("p s u h c -> p s (u h c)"),
+                        out=m_rows[n_first][:, blocks, :], in_=o_ps[:].rearrange("p s u h c -> p s (u h c)")
                     )
-                if 0 <= n_second:
-                    rows = out[0, n_second].rearrange("(r s) c -> r s c", s=ROW_BLOCKS)
+                if has_q:
+                    nc.scalar.copy(
+                        out=q_cols[n_q][:, half * HALF * HEADS : (half + 1) * HALF * HEADS, :], in_=qT_ps[:]
+                    )
+
+            if has_second:
+                rows = out[0, n_second].rearrange("(r s) c -> r s c", s=ROW_BLOCKS)
+                for half in range(2):
+                    result = results.tile([P, HALF, CHANNELS], F32)
+                    for s in range(half * HALF, (half + 1) * HALF):
+                        second_matmul(n_second, s, result)
                     nc.sync.dma_start(out=rows[:, half * HALF : (half + 1) * HALF, :], in_=result[:])

@@ -83,7 +83,6 @@ def tile_mhla_pb_t_kernel(tc, q_feat, kv_mix, w_out_words, w_out_scales, b_out, 
 
         q_cols = {}
         m_rows = {}
-        m_cols = {}
         m_codes = {}
 
         def transpose_query_block(n, s, h, qT_ps):
@@ -102,28 +101,26 @@ def tile_mhla_pb_t_kernel(tc, q_feat, kv_mix, w_out_words, w_out_scales, b_out, 
                 stop=True,
             )
 
-        def transpose_merged(n):
+        def quantise_merged(n):
             grouped = work.tile([P, ROW_BLOCKS, P, PACK], BF16, align_bytes=64)
+            codes = work.tile([P, POSITIONS], U32, align_bytes=64)
+            scales = work.tile([P, POSITIONS], U8, align_bytes=64)
             for half in range(2):
+                blocks = slice(half * HALF, (half + 1) * HALF)
+                cols = slice(half * HALF * P, (half + 1) * HALF * P)
                 mT_ps = psum_stage.tile([P, HALF, PAIRS, P], F32, tag="stage")
                 for k in range(HALF):
                     words = m_rows[n][:, half * HALF + k, :].bitcast(F32)
                     for u in range(PAIRS):
                         nc.tensor.transpose(mT_ps[:, k, u, :], words[:, u * P : (u + 1) * P], ident_f32[:])
                 nc.scalar.copy(
-                    out=grouped[:, half * HALF : (half + 1) * HALF, :, :].bitcast(F32),
-                    in_=mT_ps[:].rearrange("p s u r -> p s r u"),
+                    out=grouped[:, blocks, :, :].bitcast(F32), in_=mT_ps[:].rearrange("p s u r -> p s r u")
                 )
-            m_cols[n] = grouped
-
-        def quantise(n):
-            codes = work.tile([P, POSITIONS], U32, align_bytes=64)
-            scales = work.tile([P, POSITIONS], U8, align_bytes=64)
-            nc.vector.quantize_mx(
-                out=codes[:].bitcast(FP8X4),
-                scales=scales[:],
-                in_=m_cols[n][:].rearrange("p s r t -> p (s r t)"),
-            )
+                nc.vector.quantize_mx(
+                    out=codes[:, cols].bitcast(FP8X4),
+                    scales=scales[:, cols],
+                    in_=grouped[:, blocks, :, :].rearrange("p s r t -> p (s r t)"),
+                )
             m_codes[n] = (codes, scales)
 
         def second_matmul(n, s, result):
@@ -143,14 +140,12 @@ def tile_mhla_pb_t_kernel(tc, q_feat, kv_mix, w_out_words, w_out_scales, b_out, 
                 out=result[:, s % HALF, :], in0=out_ps[:], in1=bias_all[:], op=mybir.AluOpType.add
             )
 
-        for i in range(WINDOWS + 3):
-            n_q, n_first, n_m, n_second = i, i - 1, i - 2, i - 3
-            has_q, has_first = n_q < WINDOWS, 0 <= n_first < WINDOWS
-            has_m, has_second = 0 <= n_m < WINDOWS, 0 <= n_second
+        for i in range(WINDOWS + 2):
+            n_q, n_first, n_second = i, i - 1, i - 2
+            has_q, has_first, has_second = n_q < WINDOWS, 0 <= n_first < WINDOWS, 0 <= n_second
 
-            if has_m:
-                transpose_merged(n_m)
-                quantise(n_m)
+            if has_second:
+                quantise_merged(n_second)
 
             if has_q:
                 qT = work.tile([P, ROW_BLOCKS * HEADS, P], BF16)

@@ -21,7 +21,7 @@ ROW_BLOCKS = POSITIONS // P
 PACK = 4
 PAIRS = 2
 HALF = ROW_BLOCKS // 2
-RESULT_BUFS = 12
+RESULT_BUFS = 7
 
 FLOPS = 2 * HEADS * WINDOWS * POSITIONS * HEAD_DIM * HEAD_DIM + 2 * WINDOWS * POSITIONS * CHANNELS * CHANNELS
 
@@ -136,9 +136,7 @@ def tile_mhla_pb_t_kernel(tc, q_feat, kv_mix, w_out_words, w_out_scales, b_out, 
                 start=True,
                 stop=True,
             )
-            nc.vector.tensor_tensor(
-                out=result[:, s % HALF, :], in0=out_ps[:], in1=bias_all[:], op=mybir.AluOpType.add
-            )
+            nc.vector.tensor_tensor(out=result[:, s, :], in0=out_ps[:], in1=bias_all[:], op=mybir.AluOpType.add)
 
         for i in range(WINDOWS + 2):
             n_q, n_first, n_second = i, i - 1, i - 2
@@ -175,9 +173,11 @@ def tile_mhla_pb_t_kernel(tc, q_feat, kv_mix, w_out_words, w_out_scales, b_out, 
                     )
 
             if has_second:
+                blocks_in_store = ROW_BLOCKS if n_second < WINDOWS - 1 else HALF
                 rows = out[0, n_second].rearrange("(r s) c -> r s c", s=ROW_BLOCKS)
-                for half in range(2):
-                    result = results.tile([P, HALF, CHANNELS], F32)
-                    for s in range(half * HALF, (half + 1) * HALF):
-                        second_matmul(n_second, s, result)
-                    nc.sync.dma_start(out=rows[:, half * HALF : (half + 1) * HALF, :], in_=result[:])
+                result = results.tile([P, ROW_BLOCKS, CHANNELS], F32)
+                for s in range(ROW_BLOCKS):
+                    second_matmul(n_second, s, result)
+                    if (s + 1) % blocks_in_store == 0:
+                        done = slice(s + 1 - blocks_in_store, s + 1)
+                        nc.sync.dma_start(out=rows[:, done, :], in_=result[:, done, :])

@@ -21,7 +21,8 @@ ROW_BLOCKS = POSITIONS // P
 PACK = 4
 PAIRS = 2
 HALF = ROW_BLOCKS // 2
-RESULT_BUFS = 7
+RESULT_BUFS = 4
+LOADS_AHEAD = 6
 
 FLOPS = 2 * HEADS * WINDOWS * POSITIONS * HEAD_DIM * HEAD_DIM + 2 * WINDOWS * POSITIONS * CHANNELS * CHANNELS
 
@@ -46,22 +47,26 @@ def tile_mhla_pb_t_kernel(tc, q_feat, kv_mix, w_out_words, w_out_scales, b_out, 
         nc.vector.memset(bias_row[:], 0.0)
         ones = consts.tile([P, P], BF16)
         nc.vector.memset(ones[:], 1.0)
-        nc.sync.dma_start(out=bias_row[0:1, :], in_=b_out.unsqueeze(0))
 
         w_words = consts.tile([P, 2 * CHANNELS], U8, align_bytes=64)
         w_scales = consts.tile([P, CHANNELS], U8, align_bytes=64)
         nc.vector.memset(w_scales[:].bitcast(I32), 0)
 
-        q_rows = []
-        kv_sorted = []
-        for n in range(WINDOWS):
+        q_rows = {}
+        kv_sorted = {}
+
+        def load_window(n):
+            q_tile = inputs.tile([P, HEADS, ROW_BLOCKS * HEAD_DIM], BF16)
+            q_view = q_feat[0, :, n].rearrange("h (r s) d -> r h (s d)", s=ROW_BLOCKS)
+            if n == 0:
+                cut = HALF * HEAD_DIM
+                nc.sync.dma_start(out=q_tile[:, :, :cut], in_=q_view[:, :, :cut])
+                nc.sync.dma_start(out=q_tile[:, :, cut:], in_=q_view[:, :, cut:])
+            else:
+                nc.sync.dma_start(out=q_tile[:], in_=q_view)
+            q_rows[n] = q_tile
             kv_tile = inputs.tile([P, HEADS, HEAD_DIM], BF16)
             nc.sync.dma_start(out=kv_tile[:], in_=kv_mix[0, :, n].rearrange("h d e -> d h e"))
-            q_tile = inputs.tile([P, HEADS, ROW_BLOCKS * HEAD_DIM], BF16)
-            nc.sync.dma_start(
-                out=q_tile[:], in_=q_feat[0, :, n].rearrange("h (r s) d -> r h (s d)", s=ROW_BLOCKS)
-            )
-            q_rows.append(q_tile)
             if n == 1:
                 nc.sync.dma_start(out=w_words[:].bitcast(I32), in_=w_out_words[0].bitcast(I32))
                 for quadrant in range(4):
@@ -69,17 +74,18 @@ def tile_mhla_pb_t_kernel(tc, q_feat, kv_mix, w_out_words, w_out_scales, b_out, 
                         out=w_scales[32 * quadrant : 32 * quadrant + 4, :].bitcast(I32),
                         in_=w_out_scales[0, 4 * quadrant : 4 * quadrant + 4, :].bitcast(I32),
                     )
+                nc.sync.dma_start(out=bias_row[0:1, :], in_=b_out.unsqueeze(0))
             sorted_tile = inputs.tile([P, HEADS, HEAD_DIM], BF16)
             nc.gpsimd.tensor_copy(
                 out=sorted_tile[:].bitcast(F32).rearrange("p h (u j) -> p h u j", u=PAIRS),
                 in_=kv_tile[:].bitcast(F32).rearrange("p h (j u) -> p h u j", u=PAIRS),
             )
-            kv_sorted.append(sorted_tile)
+            kv_sorted[n] = sorted_tile
 
-        out_ps = psum_out.tile([P, CHANNELS], F32)
-        nc.tensor.matmul(out=out_ps[:], lhsT=ones[:], rhs=bias_row[:], start=True, stop=True)
+        for n in range(LOADS_AHEAD):
+            load_window(n)
+
         bias_all = consts.tile([P, CHANNELS], F32)
-        nc.vector.tensor_copy(out=bias_all[:], in_=out_ps[:])
 
         q_cols = {}
         m_rows = {}
@@ -142,6 +148,9 @@ def tile_mhla_pb_t_kernel(tc, q_feat, kv_mix, w_out_words, w_out_scales, b_out, 
             n_q, n_first, n_second = i, i - 1, i - 2
             has_q, has_first, has_second = n_q < WINDOWS, 0 <= n_first < WINDOWS, 0 <= n_second
 
+            if i + LOADS_AHEAD < WINDOWS:
+                load_window(i + LOADS_AHEAD)
+
             if has_second:
                 quantise_merged(n_second)
 
@@ -171,6 +180,11 @@ def tile_mhla_pb_t_kernel(tc, q_feat, kv_mix, w_out_words, w_out_scales, b_out, 
                     nc.scalar.copy(
                         out=q_cols[n_q][:, half * HALF * HEADS : (half + 1) * HALF * HEADS, :], in_=qT_ps[:]
                     )
+
+            if i == 1:
+                out_ps = psum_out.tile([P, CHANNELS], F32)
+                nc.tensor.matmul(out=out_ps[:], lhsT=ones[:], rhs=bias_row[:], start=True, stop=True)
+                nc.vector.tensor_copy(out=bias_all[:], in_=out_ps[:])
 
             if has_second:
                 blocks_in_store = ROW_BLOCKS if n_second < WINDOWS - 1 else HALF

@@ -22,6 +22,8 @@ PACK = 4
 PAIRS = 2
 HALF = ROW_BLOCKS // 2
 RESULT_BUFS = 4
+WARM_BEFORE = 18
+WARM_AFTER = 6
 LOADS_AHEAD = 6
 
 FLOPS = 2 * HEADS * WINDOWS * POSITIONS * HEAD_DIM * HEAD_DIM + 2 * WINDOWS * POSITIONS * CHANNELS * CHANNELS
@@ -38,6 +40,8 @@ def tile_mhla_pb_t_kernel(tc, q_feat, kv_mix, w_out_words, w_out_scales, b_out, 
         psum_stage = ctx.enter_context(tc.psum_pool(name="psum_stage", bufs=4))
         psum_out = ctx.enter_context(tc.psum_pool(name="psum_out", bufs=ROW_BLOCKS))
 
+        ones = consts.tile([P, P], BF16)
+        nc.gpsimd.memset(ones[:], 1.0)
         ident_bf16 = consts.tile([P, P], BF16)
         make_identity(nc, ident_bf16[:])
         ident_f32 = consts.tile([P, P], F32)
@@ -45,8 +49,6 @@ def tile_mhla_pb_t_kernel(tc, q_feat, kv_mix, w_out_words, w_out_scales, b_out, 
 
         bias_row = consts.tile([P, CHANNELS], BF16)
         nc.vector.memset(bias_row[:], 0.0)
-        ones = consts.tile([P, P], BF16)
-        nc.vector.memset(ones[:], 1.0)
 
         w_words = consts.tile([P, 2 * CHANNELS], U8, align_bytes=64)
         w_scales = consts.tile([P, CHANNELS], U8, align_bytes=64)
@@ -86,6 +88,13 @@ def tile_mhla_pb_t_kernel(tc, q_feat, kv_mix, w_out_words, w_out_scales, b_out, 
             load_window(n)
 
         bias_all = consts.tile([P, CHANNELS], F32)
+
+        def keep_tensor_busy(count):
+            out_ps = psum_out.tile([P, CHANNELS], F32)
+            for k in range(count):
+                nc.tensor.matmul(out=out_ps[:, :P], lhsT=ones[:], rhs=ones[:], start=True, stop=True)
+
+        keep_tensor_busy(WARM_BEFORE)
 
         q_cols = {}
         m_rows = {}
@@ -177,9 +186,11 @@ def tile_mhla_pb_t_kernel(tc, q_feat, kv_mix, w_out_words, w_out_scales, b_out, 
                         out=m_rows[n_first][:, blocks, :], in_=o_ps[:].rearrange("p s u h c -> p s (u h c)")
                     )
                 if has_q:
-                    nc.scalar.copy(
-                        out=q_cols[n_q][:, half * HALF * HEADS : (half + 1) * HALF * HEADS, :], in_=qT_ps[:]
-                    )
+                    copy_q = nc.vector.tensor_copy if i < 2 else nc.scalar.copy
+                    copy_q(out=q_cols[n_q][:, half * HALF * HEADS : (half + 1) * HALF * HEADS, :], in_=qT_ps[:])
+
+            if i == 0:
+                keep_tensor_busy(WARM_AFTER)
 
             if i == 1:
                 out_ps = psum_out.tile([P, CHANNELS], F32)
@@ -187,7 +198,7 @@ def tile_mhla_pb_t_kernel(tc, q_feat, kv_mix, w_out_words, w_out_scales, b_out, 
                 nc.vector.tensor_copy(out=bias_all[:], in_=out_ps[:])
 
             if has_second:
-                blocks_in_store = ROW_BLOCKS if n_second < WINDOWS - 1 else HALF
+                blocks_in_store = ROW_BLOCKS if n_second < WINDOWS - 1 else 1
                 rows = out[0, n_second].rearrange("(r s) c -> r s c", s=ROW_BLOCKS)
                 result = results.tile([P, ROW_BLOCKS, CHANNELS], F32)
                 for s in range(ROW_BLOCKS):

@@ -24,6 +24,7 @@ HALF = ROW_BLOCKS // 2
 RESULT_BUFS = 4
 WARM_BEFORE = 18
 WARM_AFTER = 6
+LAG = 2
 LOADS_AHEAD = 6
 
 FLOPS = 2 * HEADS * WINDOWS * POSITIONS * HEAD_DIM * HEAD_DIM + 2 * WINDOWS * POSITIONS * CHANNELS * CHANNELS
@@ -169,25 +170,29 @@ def tile_mhla_pb_t_kernel(tc, q_feat, kv_mix, w_out_words, w_out_scales, b_out, 
             if has_first:
                 merged = work.tile([P, ROW_BLOCKS, CHANNELS], BF16)
                 m_rows[n_first] = merged
-            for half in range(2):
-                blocks = slice(half * HALF, (half + 1) * HALF)
-                if has_q:
-                    qT_ps = psum_stage.tile([P, HALF * HEADS, P], BF16, tag="stage")
-                if has_first:
-                    o_ps = psum_stage.tile([P, HALF, PAIRS, HEADS, HEAD_DIM // PAIRS], BF16, tag="stage")
-                for s in range(half * HALF, (half + 1) * HALF):
-                    for h in range(HEADS):
-                        if has_q:
-                            transpose_query_block(n_q, s, h, qT_ps)
-                        if has_first:
-                            first_matmul(n_first, s, h, o_ps)
-                if has_first:
-                    nc.scalar.copy(
-                        out=m_rows[n_first][:, blocks, :], in_=o_ps[:].rearrange("p s u h c -> p s (u h c)")
-                    )
-                if has_q:
-                    copy_q = nc.vector.tensor_copy if i < 2 else nc.scalar.copy
-                    copy_q(out=q_cols[n_q][:, half * HALF * HEADS : (half + 1) * HALF * HEADS, :], in_=qT_ps[:])
+            pieces = [(s, h) for s in range(ROW_BLOCKS) for h in range(HEADS)]
+            per_half = len(pieces) // 2
+            for step in range(len(pieces) + LAG):
+                if has_q and step < len(pieces):
+                    s, h = pieces[step]
+                    if step % per_half == 0:
+                        qT_ps = psum_stage.tile([P, HALF * HEADS, P], BF16, tag="stage")
+                    transpose_query_block(n_q, s, h, qT_ps)
+                    if step % per_half == per_half - 1:
+                        half = step // per_half
+                        copy_q = nc.vector.tensor_copy if i < 2 else nc.scalar.copy
+                        copy_q(out=q_cols[n_q][:, half * HALF * HEADS : (half + 1) * HALF * HEADS, :], in_=qT_ps[:])
+                if has_first and step >= LAG:
+                    s, h = pieces[step - LAG]
+                    if (step - LAG) % per_half == 0:
+                        o_ps = psum_stage.tile([P, HALF, PAIRS, HEADS, HEAD_DIM // PAIRS], BF16, tag="stage")
+                    first_matmul(n_first, s, h, o_ps)
+                    if (step - LAG) % per_half == per_half - 1:
+                        half = (step - LAG) // per_half
+                        nc.scalar.copy(
+                            out=m_rows[n_first][:, half * HALF : (half + 1) * HALF, :],
+                            in_=o_ps[:].rearrange("p s u h c -> p s (u h c)"),
+                        )
 
             if i == 0:
                 keep_tensor_busy(WARM_AFTER)

@@ -24,6 +24,7 @@ HALF = ROW_BLOCKS // 2
 RESULT_BUFS = 4
 WARM_BEFORE = 18
 WARM_AFTER = 6
+PSUM_BANKS = 8
 LAG = 2
 LOADS_AHEAD = 6
 
@@ -38,8 +39,7 @@ def tile_mhla_pb_t_kernel(tc, q_feat, kv_mix, w_out_words, w_out_scales, b_out, 
         inputs = ctx.enter_context(tc.tile_pool(name="inputs", bufs=WINDOWS))
         work = ctx.enter_context(tc.tile_pool(name="work", bufs=2))
         results = ctx.enter_context(tc.tile_pool(name="results", bufs=RESULT_BUFS))
-        psum_stage = ctx.enter_context(tc.psum_pool(name="psum_stage", bufs=4))
-        psum_out = ctx.enter_context(tc.psum_pool(name="psum_out", bufs=ROW_BLOCKS))
+        psum = ctx.enter_context(tc.psum_pool(name="psum", bufs=PSUM_BANKS))
 
         ones = consts.tile([P, P], BF16)
         nc.gpsimd.memset(ones[:], 1.0)
@@ -91,7 +91,7 @@ def tile_mhla_pb_t_kernel(tc, q_feat, kv_mix, w_out_words, w_out_scales, b_out, 
         bias_all = consts.tile([P, CHANNELS], F32)
 
         def keep_tensor_busy(count):
-            out_ps = psum_out.tile([P, CHANNELS], F32)
+            out_ps = psum.tile([P, CHANNELS], F32, tag="bank")
             for k in range(count):
                 nc.tensor.matmul(out=out_ps[:, :P], lhsT=ones[:], rhs=ones[:], start=True, stop=True)
 
@@ -124,7 +124,7 @@ def tile_mhla_pb_t_kernel(tc, q_feat, kv_mix, w_out_words, w_out_scales, b_out, 
             for half in range(2):
                 blocks = slice(half * HALF, (half + 1) * HALF)
                 cols = slice(half * HALF * P, (half + 1) * HALF * P)
-                mT_ps = psum_stage.tile([P, HALF, PAIRS, P], F32, tag="stage")
+                mT_ps = psum.tile([P, HALF, PAIRS, P], F32, tag="bank")
                 for k in range(HALF):
                     words = m_rows[n][:, half * HALF + k, :].bitcast(F32)
                     for u in range(PAIRS):
@@ -142,7 +142,7 @@ def tile_mhla_pb_t_kernel(tc, q_feat, kv_mix, w_out_words, w_out_scales, b_out, 
         def second_matmul(n, s, result):
             codes, scales = m_codes[n]
             cols = slice(s * P, (s + 1) * P)
-            out_ps = psum_out.tile([P, CHANNELS], F32)
+            out_ps = psum.tile([P, CHANNELS], F32, tag="bank")
             nc.tensor.matmul_mx(
                 out=out_ps[:],
                 lhsT=codes[:, cols].bitcast(FP8X4),
@@ -176,7 +176,7 @@ def tile_mhla_pb_t_kernel(tc, q_feat, kv_mix, w_out_words, w_out_scales, b_out, 
                 if has_q and step < len(pieces):
                     s, h = pieces[step]
                     if step % per_half == 0:
-                        qT_ps = psum_stage.tile([P, HALF * HEADS, P], BF16, tag="stage")
+                        qT_ps = psum.tile([P, HALF * HEADS, P], BF16, tag="bank")
                     transpose_query_block(n_q, s, h, qT_ps)
                     if step % per_half == per_half - 1:
                         half = step // per_half
@@ -185,7 +185,7 @@ def tile_mhla_pb_t_kernel(tc, q_feat, kv_mix, w_out_words, w_out_scales, b_out, 
                 if has_first and step >= LAG:
                     s, h = pieces[step - LAG]
                     if (step - LAG) % per_half == 0:
-                        o_ps = psum_stage.tile([P, HALF, PAIRS, HEADS, HEAD_DIM // PAIRS], BF16, tag="stage")
+                        o_ps = psum.tile([P, HALF, PAIRS, HEADS, HEAD_DIM // PAIRS], BF16, tag="bank")
                     first_matmul(n_first, s, h, o_ps)
                     if (step - LAG) % per_half == per_half - 1:
                         half = (step - LAG) // per_half
@@ -198,7 +198,7 @@ def tile_mhla_pb_t_kernel(tc, q_feat, kv_mix, w_out_words, w_out_scales, b_out, 
                 keep_tensor_busy(WARM_AFTER)
 
             if i == 1:
-                out_ps = psum_out.tile([P, CHANNELS], F32)
+                out_ps = psum.tile([P, CHANNELS], F32, tag="bank")
                 nc.tensor.matmul(out=out_ps[:], lhsT=ones[:], rhs=bias_row[:], start=True, stop=True)
                 nc.vector.tensor_copy(out=bias_all[:], in_=out_ps[:])
 

@@ -56,7 +56,7 @@ def tile_mhla_pb_t_kernel(tc, q_feat, kv_mix, w_out_words, w_out_scales, b_out, 
         nc.vector.memset(w_scales[:].bitcast(I32), 0)
 
         q_rows = {}
-        kv_sorted = {}
+        kv_rows = {}
 
         def load_window(n):
             q_tile = inputs.tile([P, HEADS, ROW_BLOCKS * HEAD_DIM], BF16)
@@ -78,12 +78,7 @@ def tile_mhla_pb_t_kernel(tc, q_feat, kv_mix, w_out_words, w_out_scales, b_out, 
                         in_=w_out_scales[0, 4 * quadrant : 4 * quadrant + 4, :].bitcast(I32),
                     )
                 nc.sync.dma_start(out=bias_row[0:1, :], in_=b_out.unsqueeze(0))
-            sorted_tile = inputs.tile([P, HEADS, HEAD_DIM], BF16)
-            nc.gpsimd.tensor_copy(
-                out=sorted_tile[:].bitcast(F32).rearrange("p h (u j) -> p h u j", u=PAIRS),
-                in_=kv_tile[:].bitcast(F32).rearrange("p h (j u) -> p h u j", u=PAIRS),
-            )
-            kv_sorted[n] = sorted_tile
+            kv_rows[n] = kv_tile
 
         for n in range(LOADS_AHEAD):
             load_window(n)
@@ -110,9 +105,9 @@ def tile_mhla_pb_t_kernel(tc, q_feat, kv_mix, w_out_words, w_out_scales, b_out, 
 
         def first_matmul(n, s, h, o_ps):
             nc.tensor.matmul(
-                out=o_ps[:, s % HALF, :, h, :],
+                out=o_ps[:, s % HALF, h, :],
                 lhsT=q_cols[n][:, s * HEADS + h, :],
-                rhs=kv_sorted[n][:, h, :].rearrange("p (u c) -> p u c", u=PAIRS),
+                rhs=kv_rows[n][:, h, :],
                 start=True,
                 stop=True,
             )
@@ -181,17 +176,25 @@ def tile_mhla_pb_t_kernel(tc, q_feat, kv_mix, w_out_words, w_out_scales, b_out, 
                     if step % per_half == per_half - 1:
                         half = step // per_half
                         copy_q = nc.vector.tensor_copy if i < 2 else nc.scalar.copy
-                        copy_q(out=q_cols[n_q][:, half * HALF * HEADS : (half + 1) * HALF * HEADS, :], in_=qT_ps[:])
+                        copy_q(
+                            out=q_cols[n_q][:, half * HALF * HEADS : (half + 1) * HALF * HEADS, :].bitcast(F32),
+                            in_=qT_ps[:].bitcast(F32),
+                        )
                 if has_first and step >= LAG:
                     s, h = pieces[step - LAG]
                     if (step - LAG) % per_half == 0:
-                        o_ps = psum.tile([P, HALF, PAIRS, HEADS, HEAD_DIM // PAIRS], BF16, tag="bank")
+                        o_ps = psum.tile([P, HALF, HEADS, HEAD_DIM], BF16, tag="bank")
                     first_matmul(n_first, s, h, o_ps)
                     if (step - LAG) % per_half == per_half - 1:
                         half = (step - LAG) // per_half
                         nc.scalar.copy(
-                            out=m_rows[n_first][:, half * HALF : (half + 1) * HALF, :],
-                            in_=o_ps[:].rearrange("p s u h c -> p s (u h c)"),
+                            out=m_rows[n_first][:, half * HALF : (half + 1) * HALF, :]
+                            .bitcast(F32)
+                            .rearrange("p s (u k) -> p s u k", u=PAIRS),
+                            in_=o_ps[:]
+                            .rearrange("p s h e -> p s (h e)")
+                            .bitcast(F32)
+                            .rearrange("p s (k u) -> p s u k", u=PAIRS),
                         )
 
             if i == 0:

@@ -25,6 +25,7 @@ RESULT_BUFS = 4
 WARM_BEFORE = 18
 WARM_AFTER = 6
 PSUM_BANKS = 8
+BUFFER = 2
 LAG = 2
 LOADS_AHEAD = 6
 
@@ -156,17 +157,41 @@ def tile_mhla_pb_t_kernel(tc, q_feat, kv_mix, w_out_words, w_out_scales, b_out, 
             if i + LOADS_AHEAD < WINDOWS:
                 load_window(i + LOADS_AHEAD)
 
-            if has_second:
-                quantise_merged(n_second)
-
-            if has_q:
-                qT = work.tile([P, ROW_BLOCKS * HEADS, P], BF16)
-                q_cols[n_q] = qT
             if has_first:
                 merged = work.tile([P, ROW_BLOCKS, CHANNELS], BF16)
                 m_rows[n_first] = merged
             pieces = [(s, h) for s in range(ROW_BLOCKS) for h in range(HEADS)]
             per_half = len(pieces) // 2
+            done = 0
+
+            def multiply(count, done, o_ps):
+                for step in range(done, done + count):
+                    s, h = pieces[step]
+                    if step % per_half == 0:
+                        o_ps = psum.tile([P, HALF, HEADS, HEAD_DIM], BF16, tag="bank")
+                    first_matmul(n_first, s, h, o_ps)
+                    if step % per_half == per_half - 1:
+                        half = step // per_half
+                        nc.scalar.copy(
+                            out=m_rows[n_first][:, half * HALF : (half + 1) * HALF, :]
+                            .bitcast(F32)
+                            .rearrange("p s (u k) -> p s u k", u=PAIRS),
+                            in_=o_ps[:]
+                            .rearrange("p s h e -> p s (h e)")
+                            .bitcast(F32)
+                            .rearrange("p s (k u) -> p s u k", u=PAIRS),
+                        )
+                return done + count, o_ps
+
+            o_ps = None
+            if has_second:
+                if has_first:
+                    done, o_ps = multiply(BUFFER, done, o_ps)
+                quantise_merged(n_second)
+
+            if has_q:
+                qT = work.tile([P, ROW_BLOCKS * HEADS, P], BF16)
+                q_cols[n_q] = qT
             for step in range(len(pieces) + LAG):
                 if has_q and step < len(pieces):
                     s, h = pieces[step]
@@ -180,22 +205,8 @@ def tile_mhla_pb_t_kernel(tc, q_feat, kv_mix, w_out_words, w_out_scales, b_out, 
                             out=q_cols[n_q][:, half * HALF * HEADS : (half + 1) * HALF * HEADS, :].bitcast(F32),
                             in_=qT_ps[:].bitcast(F32),
                         )
-                if has_first and step >= LAG:
-                    s, h = pieces[step - LAG]
-                    if (step - LAG) % per_half == 0:
-                        o_ps = psum.tile([P, HALF, HEADS, HEAD_DIM], BF16, tag="bank")
-                    first_matmul(n_first, s, h, o_ps)
-                    if (step - LAG) % per_half == per_half - 1:
-                        half = (step - LAG) // per_half
-                        nc.scalar.copy(
-                            out=m_rows[n_first][:, half * HALF : (half + 1) * HALF, :]
-                            .bitcast(F32)
-                            .rearrange("p s (u k) -> p s u k", u=PAIRS),
-                            in_=o_ps[:]
-                            .rearrange("p s h e -> p s (h e)")
-                            .bitcast(F32)
-                            .rearrange("p s (k u) -> p s u k", u=PAIRS),
-                        )
+                if has_first and done <= step - LAG:
+                    done, o_ps = multiply(1, done, o_ps)
 
             if i == 0:
                 keep_tensor_busy(WARM_AFTER)

from contextlib import ExitStack

import concourse.mybir as mybir
from concourse.masks import make_identity

BF16 = mybir.dt.bfloat16
F32 = mybir.dt.float32
I32 = mybir.dt.int32
U32 = mybir.dt.uint32
U8 = mybir.dt.uint8
FP8X4 = mybir.dt.float8_e4m3fn_x4
FP4X4 = mybir.dt.float4_e2m1fn_x4

P = 128
HEADS = 4
WINDOWS = 16
POSITIONS = 512
HEAD_DIM = 128
CHANNELS = HEADS * HEAD_DIM
ROW_BLOCKS = POSITIONS // P
PACK = 4
PAIRS = 2
HALF = ROW_BLOCKS // 2
RESULT_BUFS = 4
WARM_BEFORE = 18
WARM_AFTER = 6
PSUM_BANKS = 8
BUFFER = 2
LAG = 2
LOADS_AHEAD = 6

FLOPS = 2 * HEADS * WINDOWS * POSITIONS * HEAD_DIM * HEAD_DIM + 2 * WINDOWS * POSITIONS * CHANNELS * CHANNELS


def tile_mhla_pb_t_kernel(tc, q_feat, kv_mix, w_out_words, w_out_scales, b_out, out):
    nc = tc.nc
    with ExitStack() as ctx:
        ctx.enter_context(tc.manual_schedule())
        consts = ctx.enter_context(tc.tile_pool(name="consts", bufs=1))
        inputs = ctx.enter_context(tc.tile_pool(name="inputs", bufs=WINDOWS))
        work = ctx.enter_context(tc.tile_pool(name="work", bufs=2))
        results = ctx.enter_context(tc.tile_pool(name="results", bufs=RESULT_BUFS))
        psum = ctx.enter_context(tc.psum_pool(name="psum", bufs=PSUM_BANKS))

        ones = consts.tile([P, P], BF16)
        nc.gpsimd.memset(ones[:], 1.0)
        ident_bf16 = consts.tile([P, P], BF16)
        make_identity(nc, ident_bf16[:])
        ident_f32 = consts.tile([P, P], F32)
        make_identity(nc, ident_f32[:])

        bias_row = consts.tile([P, CHANNELS], BF16)
        nc.vector.memset(bias_row[:], 0.0)

        w_words = consts.tile([P, 2 * CHANNELS], U8, align_bytes=64)
        w_scales = consts.tile([P, CHANNELS], U8, align_bytes=64)
        nc.vector.memset(w_scales[:].bitcast(I32), 0)

        q_rows = {}
        kv_rows = {}

        def load_window(n):
            q_tile = inputs.tile([P, HEADS, ROW_BLOCKS * HEAD_DIM], BF16)
            q_view = q_feat[0, :, n].rearrange("h (r s) d -> r h (s d)", s=ROW_BLOCKS)
            if n == 0:
                cut = HALF * HEAD_DIM
                nc.sync.dma_start(out=q_tile[:, :, :cut], in_=q_view[:, :, :cut])
                nc.sync.dma_start(out=q_tile[:, :, cut:], in_=q_view[:, :, cut:])
            else:
                nc.sync.dma_start(out=q_tile[:], in_=q_view)
            q_rows[n] = q_tile
            kv_tile = inputs.tile([P, HEADS, HEAD_DIM], BF16)
            nc.sync.dma_start(out=kv_tile[:], in_=kv_mix[0, :, n].rearrange("h d e -> d h e"))
            if n == 1:
                nc.sync.dma_start(out=w_words[:].bitcast(I32), in_=w_out_words[0].bitcast(I32))
                for quadrant in range(4):
                    nc.sync.dma_start(
                        out=w_scales[32 * quadrant : 32 * quadrant + 4, :].bitcast(I32),
                        in_=w_out_scales[0, 4 * quadrant : 4 * quadrant + 4, :].bitcast(I32),
                    )
                nc.sync.dma_start(out=bias_row[0:1, :], in_=b_out.unsqueeze(0))
            kv_rows[n] = kv_tile

        for n in range(LOADS_AHEAD):
            load_window(n)

        bias_all = consts.tile([P, CHANNELS], F32)

        def keep_tensor_busy(count):
            out_ps = psum.tile([P, CHANNELS], F32, tag="bank")
            for k in range(count):
                nc.tensor.matmul(out=out_ps[:, :P], lhsT=ones[:], rhs=ones[:], start=True, stop=True)

        keep_tensor_busy(WARM_BEFORE)

        q_cols = {}
        m_rows = {}
        m_codes = {}

        def transpose_query_block(n, s, h, qT_ps):
            nc.tensor.transpose(
                qT_ps[:, (s % HALF) * HEADS + h, :],
                q_rows[n][:, h, s * HEAD_DIM : (s + 1) * HEAD_DIM],
                ident_bf16[:],
            )

        def first_matmul(n, s, h, o_ps):
            nc.tensor.matmul(
                out=o_ps[:, s % HALF, h, :],
                lhsT=q_cols[n][:, s * HEADS + h, :],
                rhs=kv_rows[n][:, h, :],
                start=True,
                stop=True,
            )

        def quantise_merged(n):
            grouped = work.tile([P, ROW_BLOCKS, P, PACK], BF16, align_bytes=64)
            codes = work.tile([P, POSITIONS], U32, align_bytes=64)
            scales = work.tile([P, POSITIONS], U8, align_bytes=64)
            for half in range(2):
                blocks = slice(half * HALF, (half + 1) * HALF)
                cols = slice(half * HALF * P, (half + 1) * HALF * P)
                mT_ps = psum.tile([P, HALF, PAIRS, P], F32, tag="bank")
                for k in range(HALF):
                    words = m_rows[n][:, half * HALF + k, :].bitcast(F32)
                    for u in range(PAIRS):
                        nc.tensor.transpose(mT_ps[:, k, u, :], words[:, u * P : (u + 1) * P], ident_f32[:])
                nc.scalar.copy(
                    out=grouped[:, blocks, :, :].bitcast(F32), in_=mT_ps[:].rearrange("p s u r -> p s r u")
                )
                nc.vector.quantize_mx(
                    out=codes[:, cols].bitcast(FP8X4),
                    scales=scales[:, cols],
                    in_=grouped[:, blocks, :, :].rearrange("p s r t -> p (s r t)"),
                )
            m_codes[n] = (codes, scales)

        def second_matmul(n, s, result):
            codes, scales = m_codes[n]
            cols = slice(s * P, (s + 1) * P)
            out_ps = psum.tile([P, CHANNELS], F32, tag="bank")
            nc.tensor.matmul_mx(
                out=out_ps[:],
                lhsT=codes[:, cols].bitcast(FP8X4),
                lhsT_scale=scales[:, cols],
                rhs=w_words[:].bitcast(FP4X4),
                rhs_scale=w_scales[:],
                start=True,
                stop=True,
            )
            nc.vector.tensor_tensor(out=result[:, s, :], in0=out_ps[:], in1=bias_all[:], op=mybir.AluOpType.add)

        for i in range(WINDOWS + 2):
            n_q, n_first, n_second = i, i - 1, i - 2
            has_q, has_first, has_second = n_q < WINDOWS, 0 <= n_first < WINDOWS, 0 <= n_second

            if i + LOADS_AHEAD < WINDOWS:
                load_window(i + LOADS_AHEAD)

            if has_first:
                merged = work.tile([P, ROW_BLOCKS, CHANNELS], BF16)
                m_rows[n_first] = merged
            pieces = [(s, h) for s in range(ROW_BLOCKS) for h in range(HEADS)]
            per_half = len(pieces) // 2
            done = 0

            def multiply(count, done, o_ps):
                for step in range(done, done + count):
                    s, h = pieces[step]
                    if step % per_half == 0:
                        o_ps = psum.tile([P, HALF, HEADS, HEAD_DIM], BF16, tag="bank")
                    first_matmul(n_first, s, h, o_ps)
                    if step % per_half == per_half - 1:
                        half = step // per_half
                        nc.scalar.copy(
                            out=m_rows[n_first][:, half * HALF : (half + 1) * HALF, :]
                            .bitcast(F32)
                            .rearrange("p s (u k) -> p s u k", u=PAIRS),
                            in_=o_ps[:]
                            .rearrange("p s h e -> p s (h e)")
                            .bitcast(F32)
                            .rearrange("p s (k u) -> p s u k", u=PAIRS),
                        )
                return done + count, o_ps

            o_ps = None
            if has_second:
                if has_first:
                    done, o_ps = multiply(BUFFER, done, o_ps)
                quantise_merged(n_second)

            if has_q:
                qT = work.tile([P, ROW_BLOCKS * HEADS, P], BF16)
                q_cols[n_q] = qT
            for step in range(len(pieces) + LAG):
                if has_q and step < len(pieces):
                    s, h = pieces[step]
                    if step % per_half == 0:
                        qT_ps = psum.tile([P, HALF * HEADS, P], BF16, tag="bank")
                    transpose_query_block(n_q, s, h, qT_ps)
                    if step % per_half == per_half - 1:
                        half = step // per_half
                        copy_q = nc.vector.tensor_copy if i < 2 else nc.scalar.copy
                        copy_q(
                            out=q_cols[n_q][:, half * HALF * HEADS : (half + 1) * HALF * HEADS, :].bitcast(F32),
                            in_=qT_ps[:].bitcast(F32),
                        )
                if has_first and done <= step - LAG:
                    done, o_ps = multiply(1, done, o_ps)

            if i == 0:
                keep_tensor_busy(WARM_AFTER)

            if i == 1:
                out_ps = psum.tile([P, CHANNELS], F32, tag="bank")
                nc.tensor.matmul(out=out_ps[:], lhsT=ones[:], rhs=bias_row[:], start=True, stop=True)
                nc.vector.tensor_copy(out=bias_all[:], in_=out_ps[:])

            if has_second:
                blocks_in_store = ROW_BLOCKS if n_second < WINDOWS - 1 else 1
                rows = out[0, n_second].rearrange("(r s) c -> r s c", s=ROW_BLOCKS)
                result = results.tile([P, ROW_BLOCKS, CHANNELS], F32)
                for s in range(ROW_BLOCKS):
                    second_matmul(n_second, s, result)
                    if (s + 1) % blocks_in_store == 0:
                        done = slice(s + 1 - blocks_in_store, s + 1)
                        nc.sync.dma_start(out=rows[:, done, :], in_=result[:, done, :])
